import numpy as np
import ml_dtypes


def mxq(x, axis, fmt="e4m3"):
    dtype, down = {"e4m3": (ml_dtypes.float8_e4m3fn, 7), "e5m2": (ml_dtypes.float8_e5m2, 14)}[fmt]
    v = np.moveaxis(np.asarray(x, np.float32).astype(ml_dtypes.bfloat16).astype(np.float64), axis, -1)
    blocks = v.reshape(v.shape[:-1] + (-1, 32))
    amax = np.abs(blocks).max(-1, keepdims=True)
    byte = np.maximum(np.where(amax > 0, np.frexp(amax)[1] - 1 + 127, 0) - down, 1)
    scale = np.exp2(byte - 127.0)
    codes = (blocks / scale).astype(np.float32).astype(dtype).astype(np.float64)
    return np.moveaxis((codes * scale).reshape(v.shape), -1, axis)


WIDE = False


def mx_kscale(k):
    if not WIDE:
        return np.ones(k)
    levels = np.array([10, -10, 5, -5, 0])
    if k % 512:
        return np.exp2(np.random.permutation(np.resize(levels, k // 32))).repeat(32)
    a = np.empty((k // 512, 16))
    for p in range(k // 512):
        a[p, :8] = np.random.permutation(np.resize(levels, 8))
        for g in range(8):
            far = levels[np.abs(levels - a[p, g]) >= 10]
            a[p, g + 8] = far[np.random.randint(len(far))]
    return np.exp2(a.ravel()).repeat(32)


BF16 = ml_dtypes.bfloat16


def bf(x):
    return np.asarray(x, np.float32).astype(BF16)


def f64(x):
    return np.asarray(x).astype(np.float64)


B, S, E, HID, H = 2, 4096, 512, 1024, 8
DH = HID // H


def setup_inputs():
    t = mx_kscale(HID)
    kv_rms = np.hypot(6.0 * np.sqrt(S), 0.19 * S)
    return {"q_feat": bf(1.0 + 2.8 * np.random.standard_normal((B, H, S, DH))),
            "kv": bf(np.random.standard_normal((B, H, DH, DH)) * kv_rms * t.reshape(H, 1, DH)),
            "denom": bf(S * DH * (1.0 + 0.1 * np.random.standard_normal((B, H, 1, 1)))),
            "Wo": bf(np.random.standard_normal((HID, E)) * 4.0 / np.sqrt(HID) / t[:, None]),
            "bo": bf(np.random.standard_normal(E) * 0.1)}


def reference(q_feat, kv, denom, Wo, bo):
    qkv = f64(q_feat) @ f64(kv)
    ctx = qkv / f64(denom)
    ctx = ctx.transpose(0, 2, 1, 3).reshape(B, S, HID)
    return (mxq(ctx, 2, "e4m3") @ mxq(f64(Wo), 0, "e4m3")) + f64(bo)

@@ -1,0 +1,248 @@
+from contextlib import ExitStack
+
+import concourse.masks as masks
+import concourse.mybir as mybir
+
+BF16 = mybir.dt.bfloat16
+F32 = mybir.dt.float32
+U32 = mybir.dt.uint32
+U8 = mybir.dt.uint8
+FP8X4 = mybir.dt.float8_e4m3fn_x4
+
+P = 128
+B, H, S, DH, E = 2, 8, 4096, 128, 512
+PACK = 4
+PAIRS = 2
+HEADS = 4
+PASSES = H // HEADS
+ROWS = HEADS * DH
+J = 4
+BLOCK = P * J
+BLOCKS_PER_SEQ = S // BLOCK
+N_BLOCKS = B * BLOCKS_PER_SEQ
+N_TILES = N_BLOCKS * J
+LOADS_AHEAD = 4
+
+FLOPS = 2 * B * H * S * DH * DH + 2 * B * S * H * DH * E
+
+
+def tile_linearattention_pb_t_kernel(tc, q_feat, kv, denom, Wo, bo, out):
+    nc = tc.nc
+    with ExitStack() as stack:
+        const = stack.enter_context(tc.tile_pool(name="const", bufs=1))
+        q_pool = stack.enter_context(tc.tile_pool(name="q", bufs=(LOADS_AHEAD + 2) * PASSES))
+        work = stack.enter_context(tc.tile_pool(name="work", bufs=3))
+        mx_pool = stack.enter_context(tc.tile_pool(name="mx", bufs=3))
+        out_pool = stack.enter_context(tc.tile_pool(name="outs", bufs=6))
+        qT_banks = stack.enter_context(tc.psum_pool(name="qT_banks", bufs=2))
+        ctx_banks = stack.enter_context(tc.psum_pool(name="ctx_banks", bufs=2))
+        ctxT_banks = stack.enter_context(tc.psum_pool(name="ctxT_banks", bufs=2))
+        out_banks = stack.enter_context(tc.psum_pool(name="out_banks", bufs=2))
+        stack.enter_context(tc.manual_schedule())
+
+        q_tiles = {}
+
+        def load_unit(blk, g):
+            b, part = divmod(blk, BLOCKS_PER_SEQ)
+            q_tiles[blk, g] = q_pool.tile([P, HEADS, J * DH], BF16, name="q_sb", tag="q_sb")
+            rows = q_feat[b, g * HEADS : (g + 1) * HEADS, part * BLOCK : (part + 1) * BLOCK, :]
+            nc.sync.dma_start(out=q_tiles[blk, g][:], in_=rows.rearrange("h (p j) d -> p h (j d)", j=J))
+
+        bias_row = const.tile([P, E], BF16)
+        nc.vector.memset(bias_row[:], 0.0)
+        ones = const.tile([P, P], BF16)
+        nc.vector.memset(ones[:], 1.0)
+        identity = const.tile([P, P], BF16)
+        masks.make_identity(nc, identity[:])
+        identity_f32 = const.tile([P, P], F32)
+        masks.make_identity(nc, identity_f32[:])
+
+        load_unit(0, 0)
+        kv_raw = const.tile([P, B, H * DH], BF16, align_bytes=64)
+        nc.sync.dma_start(
+            out=kv_raw[:, 0, :].rearrange("d (h e) -> d h e", h=H), in_=kv[0].rearrange("h d e -> d h e")
+        )
+        denom_bc = const.tile([P, B * H], BF16)
+        nc.sync.dma_start(out=denom_bc[:], in_=denom.rearrange("b h x y -> (b h x y)").partition_broadcast(P))
+        load_unit(0, 1)
+        nc.sync.dma_start(out=bias_row[0:1, :], in_=bo.rearrange("(o n) -> o n", o=1))
+        wo_raw = const.tile([P, PASSES, PACK, E], BF16)
+        nc.sync.dma_start(out=wo_raw[:], in_=Wo.rearrange("(g p t) n -> p g t n", p=P, t=PACK))
+        for blk in range(1, LOADS_AHEAD):
+            load_unit(blk, 0)
+            load_unit(blk, 1)
+        nc.sync.dma_start(
+            out=kv_raw[:, 1, :].rearrange("d (h e) -> d h e", h=H), in_=kv[1].rearrange("h d e -> d h e")
+        )
+
+        kv_sb = const.tile([P, B, H * DH], BF16, align_bytes=64)
+        rden = const.tile([P, B * H], F32)
+        bias_sb = const.tile([P, E], F32)
+        wo_grouped = const.tile([P, PASSES, E, PACK], BF16, align_bytes=64)
+        wo_codes = const.tile([P, PASSES, E], U32, align_bytes=64)
+        wo_scales = const.tile([P, PASSES, E], U8, align_bytes=64)
+
+        def order_kv(b):
+            nc.vector.tensor_copy(
+                out=kv_sb[:, b, :].bitcast(F32).rearrange("d (h u c) -> d h u c", h=H, u=PAIRS),
+                in_=kv_raw[:, b, :].bitcast(F32).rearrange("d (h c u) -> d h u c", h=H, u=PAIRS),
+            )
+
+        def prepare_projection():
+            bias_ps = out_banks.tile([P, E], F32, name="bias_ps", tag="out_ps")
+            nc.tensor.matmul(out=bias_ps[:], lhsT=ones[:], rhs=bias_row[:], start=True, stop=True)
+            nc.vector.tensor_copy(out=bias_sb[:], in_=bias_ps[:])
+            for g in range(PASSES):
+                nc.vector.tensor_copy(
+                    out=wo_grouped[:, g].rearrange("p (c i) t -> p c t i", i=4),
+                    in_=wo_raw[:, g].rearrange("p t (c i) -> p c t i", i=4),
+                )
+            nc.vector.quantize_mx(
+                out=wo_codes[:].rearrange("p g n -> p (g n)").bitcast(FP8X4),
+                scales=wo_scales[:].rearrange("p g n -> p (g n)"),
+                in_=wo_grouped[:].rearrange("p g n t -> p (g n t)"),
+            )
+
+        qT_ps, qT_sb, ctx_ps, ctx_sb, ctxT_ps, grouped = {}, {}, {}, {}, {}, {}
+        codes, scales, out_ps, out_sb = {}, {}, {}, {}
+
+        def is_tile(i):
+            return 0 <= i < N_TILES
+
+        def transpose_q(i):
+            blk, j = divmod(i, J)
+            qT_ps[i] = qT_banks.tile([P, H, P], BF16, name="qT_ps", tag="qT_ps")
+            for h in range(H):
+                g, hh = divmod(h, HEADS)
+                nc.tensor.transpose(
+                    qT_ps[i][:, h, :], q_tiles[blk, g][:, hh, j * DH : (j + 1) * DH], identity[:]
+                )
+
+        def copy_qT(i):
+            qT_sb[i] = work.tile([P, H, P], BF16, name="qT_sb", tag="qT_sb")
+            nc.scalar.copy(out=qT_sb[i][:], in_=qT_ps[i][:])
+
+        def plain_matmuls(i, g):
+            b = i // (J * BLOCKS_PER_SEQ)
+            ctx_ps[i, g] = ctx_banks.tile([P, HEADS, DH], F32, name="ctx_ps", tag="ctx_ps")
+            for hh in range(HEADS):
+                h = g * HEADS + hh
+                nc.tensor.matmul(
+                    out=ctx_ps[i, g][:, hh, :],
+                    lhsT=qT_sb[i][:, h, :],
+                    rhs=kv_sb[:, b, h * DH : (h + 1) * DH],
+                    start=True,
+                    stop=True,
+                )
+
+        def divide(i, g):
+            b = i // (J * BLOCKS_PER_SEQ)
+            ctx_sb[i, g] = work.tile([P, PAIRS, ROWS // PAIRS], BF16, name="ctx_sb", tag="ctx_sb%d" % g)
+            dst = ctx_sb[i, g][:].rearrange("p u (h c) -> p h u c", h=HEADS)
+            src = ctx_ps[i, g][:].rearrange("p h (u c) -> p h u c", u=PAIRS)
+            head = b * H + g * HEADS
+            if g == 0:
+                for hh in range(HEADS):
+                    nc.scalar.activation(
+                        out=dst[:, hh],
+                        in_=src[:, hh],
+                        func=mybir.ActivationFunctionType.Copy,
+                        scale=rden[:, head + hh : head + hh + 1],
+                    )
+            else:
+                nc.vector.tensor_tensor(
+                    out=dst,
+                    in0=src,
+                    in1=rden_full[:, head * DH : (head + HEADS) * DH].rearrange(
+                        "p (h u c) -> p h u c", h=HEADS, u=PAIRS
+                    ),
+                    op=mybir.AluOpType.mult,
+                )
+
+        rden_full = const.tile([P, B * H * DH], F32)
+
+        def transpose_ctx(i):
+            ctxT_ps[i] = ctxT_banks.tile([P, PASSES, PAIRS, P], F32, name="ctxT_ps", tag="ctxT_ps")
+            for g in range(PASSES):
+                for u in range(PAIRS):
+                    nc.tensor.transpose(
+                        ctxT_ps[i][:, g, u, :], ctx_sb[i, g][:, u, :].bitcast(F32), identity_f32[:]
+                    )
+
+        def regroup(i):
+            grouped[i] = work.tile([P, PASSES, P, PACK], BF16, name="grouped", tag="grouped", align_bytes=64)
+            nc.scalar.copy(
+                out=grouped[i][:].rearrange("p g s t -> p (g s t)").bitcast(F32).rearrange(
+                    "p (g s u) -> p g s u", g=PASSES, u=PAIRS
+                ),
+                in_=ctxT_ps[i][:].rearrange("p g u s -> p g s u"),
+            )
+
+        def quantise(i):
+            codes[i] = mx_pool.tile([P, PASSES, P], U32, name="codes", tag="codes", align_bytes=64)
+            scales[i] = mx_pool.tile([P, PASSES, P], U8, name="scales", tag="scales", align_bytes=64)
+            nc.vector.quantize_mx(
+                out=codes[i][:].rearrange("p g s -> p (g s)").bitcast(FP8X4),
+                scales=scales[i][:].rearrange("p g s -> p (g s)"),
+                in_=grouped[i][:].rearrange("p g s t -> p (g s t)"),
+            )
+
+        def project(i):
+            out_ps[i] = out_banks.tile([P, E], F32, name="out_ps", tag="out_ps")
+            for g in range(PASSES):
+                nc.tensor.matmul_mx(
+                    out=out_ps[i][:],
+                    lhsT=codes[i][:, g, :].bitcast(FP8X4),
+                    lhsT_scale=scales[i][:, g, :],
+                    rhs=wo_codes[:, g, :].bitcast(FP8X4),
+                    rhs_scale=wo_scales[:, g, :],
+                    start=(g == 0),
+                    stop=(g == PASSES - 1),
+                )
+
+        def add_bias_and_store(i):
+            out_sb[i] = out_pool.tile([P, E], F32, name="out_sb", tag="out_sb")
+            nc.vector.tensor_tensor(out=out_sb[i][:], in0=out_ps[i][:], in1=bias_sb[:], op=mybir.AluOpType.add)
+            blk, j = divmod(i, J)
+            b, part = divmod(blk, BLOCKS_PER_SEQ)
+            rows = out[b, part * BLOCK : (part + 1) * BLOCK, :].rearrange("(p j) n -> p j n", j=J)
+            nc.sync.dma_start(out=rows[:, j, :], in_=out_sb[i][:])
+
+        for step in range(N_TILES + 5):
+            if step == 1:
+                nc.vector.reciprocal(out=rden[:], in_=denom_bc[:])
+                nc.vector.tensor_copy(
+                    out=rden_full[:].rearrange("p (h e) -> p h e", e=DH),
+                    in_=rden[:].unsqueeze(2).to_broadcast([P, B * H, DH]),
+                )
+            if step == 0:
+                order_kv(0)
+            if is_tile(step - 1):
+                plain_matmuls(step - 1, 0)
+            if is_tile(step):
+                transpose_q(step)
+            if is_tile(step - 2):
+                transpose_ctx(step - 2)
+            if is_tile(step - 1):
+                plain_matmuls(step - 1, 1)
+            if is_tile(step - 4):
+                project(step - 4)
+
+            if is_tile(step - 5):
+                add_bias_and_store(step - 5)
+            blk, j = divmod(step - 5, J)
+            if j in (0, 2) and 0 <= blk and blk + LOADS_AHEAD < N_BLOCKS:
+                load_unit(blk + LOADS_AHEAD, j // 2)
+            if is_tile(step - 1):
+                divide(step - 1, 0)
+                divide(step - 1, 1)
+            if is_tile(step):
+                copy_qT(step)
+            if is_tile(step - 2):
+                regroup(step - 2)
+            if is_tile(step - 3):
+                quantise(step - 3)
+            if step == 2:
+                prepare_projection()
+            if step == 8:
+                order_kv(1)

@@ -21,6 +21,7 @@ BLOCK = P * J
 BLOCKS_PER_SEQ = S // BLOCK
 N_BLOCKS = B * BLOCKS_PER_SEQ
 N_TILES = N_BLOCKS * J
+VECTOR_TAKES = 3
 LOADS_AHEAD = 4
 
 FLOPS = 2 * B * H * S * DH * DH + 2 * B * S * H * DH * E
@@ -141,7 +142,7 @@ def tile_linearattention_pb_t_kernel(tc, q_feat, kv, denom, Wo, bo, out):
             dst = ctx_sb[i, g][:].rearrange("p u (h c) -> p h u c", h=HEADS)
             src = ctx_ps[i, g][:].rearrange("p h (u c) -> p h u c", u=PAIRS)
             head = b * H + g * HEADS
-            if g == 0:
+            if g == 0 and i % VECTOR_TAKES != 0:
                 for hh in range(HEADS):
                     nc.scalar.activation(
                         out=dst[:, hh],
@@ -208,41 +209,40 @@ def tile_linearattention_pb_t_kernel(tc, q_feat, kv, denom, Wo, bo, out):
             rows = out[b, part * BLOCK : (part + 1) * BLOCK, :].rearrange("(p j) n -> p j n", j=J)
             nc.sync.dma_start(out=rows[:, j, :], in_=out_sb[i][:])
 
-        for step in range(N_TILES + 5):
-            if step == 1:
+        for step in range(N_TILES + 6):
+            if step == 0:
+                order_kv(0)
                 nc.vector.reciprocal(out=rden[:], in_=denom_bc[:])
                 nc.vector.tensor_copy(
                     out=rden_full[:].rearrange("p (h e) -> p h e", e=DH),
                     in_=rden[:].unsqueeze(2).to_broadcast([P, B * H, DH]),
                 )
-            if step == 0:
-                order_kv(0)
-            if is_tile(step - 1):
-                plain_matmuls(step - 1, 0)
             if is_tile(step):
                 transpose_q(step)
             if is_tile(step - 2):
-                transpose_ctx(step - 2)
-            if is_tile(step - 1):
-                plain_matmuls(step - 1, 1)
-            if is_tile(step - 4):
-                project(step - 4)
-
+                divide(step - 2, 0)
+            if step == 4:
+                prepare_projection()
             if is_tile(step - 5):
-                add_bias_and_store(step - 5)
-            blk, j = divmod(step - 5, J)
+                quantise(step - 5)
+            if is_tile(step - 4):
+                regroup(step - 4)
+            if is_tile(step - 3):
+                transpose_ctx(step - 3)
+            if is_tile(step - 2):
+                divide(step - 2, 1)
+            if is_tile(step - 6):
+                add_bias_and_store(step - 6)
+            blk, j = divmod(step - 6, J)
             if j in (0, 2) and 0 <= blk and blk + LOADS_AHEAD < N_BLOCKS:
                 load_unit(blk + LOADS_AHEAD, j // 2)
             if is_tile(step - 1):
-                divide(step - 1, 0)
-                divide(step - 1, 1)
+                plain_matmuls(step - 1, 0)
+            if is_tile(step - 5):
+                project(step - 5)
+            if is_tile(step - 1):
+                plain_matmuls(step - 1, 1)
             if is_tile(step):
                 copy_qT(step)
-            if is_tile(step - 2):
-                regroup(step - 2)
-            if is_tile(step - 3):
-                quantise(step - 3)
-            if step == 2:
-                prepare_projection()
             if step == 8:
                 order_kv(1)

@@ -12,7 +12,7 @@ FP8X4 = mybir.dt.float8_e4m3fn_x4
 P = 128
 B, H, S, DH, E = 2, 8, 4096, 128, 512
 PACK = 4
-PAIRS = 2
+HALF = 2
 HEADS = 4
 PASSES = H // HEADS
 ROWS = HEADS * DH
@@ -20,8 +20,8 @@ J = 4
 BLOCK = P * J
 BLOCKS_PER_SEQ = S // BLOCK
 N_BLOCKS = B * BLOCKS_PER_SEQ
-N_TILES = N_BLOCKS * J
-VECTOR_TAKES = 3
+PAIRS_PER_BLOCK = 2
+N_PAIRS = N_BLOCKS * PAIRS_PER_BLOCK
 LOADS_AHEAD = 4
 
 FLOPS = 2 * B * H * S * DH * DH + 2 * B * S * H * DH * E
@@ -32,8 +32,8 @@ def tile_linearattention_pb_t_kernel(tc, q_feat, kv, denom, Wo, bo, out):
     with ExitStack() as stack:
         const = stack.enter_context(tc.tile_pool(name="const", bufs=1))
         q_pool = stack.enter_context(tc.tile_pool(name="q", bufs=(LOADS_AHEAD + 2) * PASSES))
-        work = stack.enter_context(tc.tile_pool(name="work", bufs=3))
-        mx_pool = stack.enter_context(tc.tile_pool(name="mx", bufs=3))
+        work = stack.enter_context(tc.tile_pool(name="work", bufs=4))
+        mx_pool = stack.enter_context(tc.tile_pool(name="mx", bufs=4))
         out_pool = stack.enter_context(tc.tile_pool(name="outs", bufs=6))
         qT_banks = stack.enter_context(tc.psum_pool(name="qT_banks", bufs=2))
         ctx_banks = stack.enter_context(tc.psum_pool(name="ctx_banks", bufs=2))
@@ -53,19 +53,17 @@ def tile_linearattention_pb_t_kernel(tc, q_feat, kv, denom, Wo, bo, out):
         nc.vector.memset(bias_row[:], 0.0)
         ones = const.tile([P, P], BF16)
         nc.vector.memset(ones[:], 1.0)
-        identity = const.tile([P, P], BF16)
+        identity = const.tile([P, P], F32)
         masks.make_identity(nc, identity[:])
-        identity_f32 = const.tile([P, P], F32)
-        masks.make_identity(nc, identity_f32[:])
 
         load_unit(0, 0)
         kv_raw = const.tile([P, B, H * DH], BF16, align_bytes=64)
         nc.sync.dma_start(
             out=kv_raw[:, 0, :].rearrange("d (h e) -> d h e", h=H), in_=kv[0].rearrange("h d e -> d h e")
         )
+        load_unit(0, 1)
         denom_bc = const.tile([P, B * H], BF16)
         nc.sync.dma_start(out=denom_bc[:], in_=denom.rearrange("b h x y -> (b h x y)").partition_broadcast(P))
-        load_unit(0, 1)
         nc.sync.dma_start(out=bias_row[0:1, :], in_=bo.rearrange("(o n) -> o n", o=1))
         wo_raw = const.tile([P, PASSES, PACK, E], BF16)
         nc.sync.dma_start(out=wo_raw[:], in_=Wo.rearrange("(g p t) n -> p g t n", p=P, t=PACK))
@@ -78,6 +76,7 @@ def tile_linearattention_pb_t_kernel(tc, q_feat, kv, denom, Wo, bo, out):
 
         kv_sb = const.tile([P, B, H * DH], BF16, align_bytes=64)
         rden = const.tile([P, B * H], F32)
+        rden_full = const.tile([P, B * H * DH], F32)
         bias_sb = const.tile([P, E], F32)
         wo_grouped = const.tile([P, PASSES, E, PACK], BF16, align_bytes=64)
         wo_codes = const.tile([P, PASSES, E], U32, align_bytes=64)
@@ -85,8 +84,15 @@ def tile_linearattention_pb_t_kernel(tc, q_feat, kv, denom, Wo, bo, out):
 
         def order_kv(b):
             nc.vector.tensor_copy(
-                out=kv_sb[:, b, :].bitcast(F32).rearrange("d (h u c) -> d h u c", h=H, u=PAIRS),
-                in_=kv_raw[:, b, :].bitcast(F32).rearrange("d (h c u) -> d h u c", h=H, u=PAIRS),
+                out=kv_sb[:, b, :].bitcast(F32).rearrange("d (h u c) -> d h u c", h=H, u=HALF),
+                in_=kv_raw[:, b, :].bitcast(F32).rearrange("d (h c u) -> d h u c", h=H, u=HALF),
+            )
+
+        def prepare_division():
+            nc.vector.reciprocal(out=rden[:], in_=denom_bc[:])
+            nc.vector.tensor_copy(
+                out=rden_full[:].rearrange("p (h e) -> p h e", e=DH),
+                in_=rden[:].unsqueeze(2).to_broadcast([P, B * H, DH]),
             )
 
         def prepare_projection():
@@ -104,45 +110,59 @@ def tile_linearattention_pb_t_kernel(tc, q_feat, kv, denom, Wo, bo, out):
                 in_=wo_grouped[:].rearrange("p g n t -> p (g n t)"),
             )
 
-        qT_ps, qT_sb, ctx_ps, ctx_sb, ctxT_ps, grouped = {}, {}, {}, {}, {}, {}
+        q_pairs, qT_ps, qT_sb, ctx_ps, ctx_sb, ctxT_ps, grouped = {}, {}, {}, {}, {}, {}, {}
         codes, scales, out_ps, out_sb = {}, {}, {}, {}
 
-        def is_tile(i):
-            return 0 <= i < N_TILES
-
-        def transpose_q(i):
-            blk, j = divmod(i, J)
-            qT_ps[i] = qT_banks.tile([P, H, P], BF16, name="qT_ps", tag="qT_ps")
-            for h in range(H):
-                g, hh = divmod(h, HEADS)
-                nc.tensor.transpose(
-                    qT_ps[i][:, h, :], q_tiles[blk, g][:, hh, j * DH : (j + 1) * DH], identity[:]
+        def pair_queries(s, g):
+            blk, l = divmod(s, PAIRS_PER_BLOCK)
+            q_pairs[s, g] = work.tile([P, HEADS, DH, HALF], BF16, name="q_pairs", tag="q_pairs", align_bytes=64)
+            src = q_tiles[blk, g][:].rearrange("p h (r l d) -> p l h d r", r=HALF, l=PAIRS_PER_BLOCK)[:, l]
+            if g == 0:
+                nc.gpsimd.tensor_scalar(
+                    out=q_pairs[s, g][:],
+                    in0=src,
+                    scalar1=1.0,
+                    scalar2=0.0,
+                    op0=mybir.AluOpType.mult,
+                    op1=mybir.AluOpType.add,
                 )
+            else:
+                nc.vector.tensor_copy(out=q_pairs[s, g][:], in_=src)
 
-        def copy_qT(i):
-            qT_sb[i] = work.tile([P, H, P], BF16, name="qT_sb", tag="qT_sb")
-            nc.scalar.copy(out=qT_sb[i][:], in_=qT_ps[i][:])
-
-        def plain_matmuls(i, g):
-            b = i // (J * BLOCKS_PER_SEQ)
-            ctx_ps[i, g] = ctx_banks.tile([P, HEADS, DH], F32, name="ctx_ps", tag="ctx_ps")
+        def transpose_q(s, g):
+            qT_ps[s, g] = qT_banks.tile([P, HEADS, P], F32, name="qT_ps", tag="qT_ps")
+            words = q_pairs[s, g][:].rearrange("p h d r -> p (h d r)").bitcast(F32)
             for hh in range(HEADS):
-                h = g * HEADS + hh
-                nc.tensor.matmul(
-                    out=ctx_ps[i, g][:, hh, :],
-                    lhsT=qT_sb[i][:, h, :],
-                    rhs=kv_sb[:, b, h * DH : (h + 1) * DH],
-                    start=True,
-                    stop=True,
-                )
+                nc.tensor.transpose(qT_ps[s, g][:, hh, :], words[:, hh * P : (hh + 1) * P], identity[:])
 
-        def divide(i, g):
-            b = i // (J * BLOCKS_PER_SEQ)
-            ctx_sb[i, g] = work.tile([P, PAIRS, ROWS // PAIRS], BF16, name="ctx_sb", tag="ctx_sb%d" % g)
-            dst = ctx_sb[i, g][:].rearrange("p u (h c) -> p h u c", h=HEADS)
-            src = ctx_ps[i, g][:].rearrange("p h (u c) -> p h u c", u=PAIRS)
+        def copy_qT(s, g):
+            qT_sb[s, g] = work.tile([P, HEADS, HALF * P], BF16, name="qT_sb", tag="qT_sb", align_bytes=64)
+            nc.scalar.copy(
+                out=qT_sb[s, g][:].rearrange("d h m -> d (h m)").bitcast(F32),
+                in_=qT_ps[s, g][:].rearrange("d h p -> d (h p)"),
+            )
+
+        def plain_matmuls(s, c):
+            b = s // (PAIRS_PER_BLOCK * BLOCKS_PER_SEQ)
+            for g in range(PASSES):
+                ctx_ps[s, c, g] = ctx_banks.tile([P, HEADS, DH], F32, name="ctx_ps", tag="ctx_ps")
+                for hh in range(HEADS):
+                    h = g * HEADS + hh
+                    nc.tensor.matmul(
+                        out=ctx_ps[s, c, g][:, hh, :],
+                        lhsT=qT_sb[s, g][:, hh, c * P : (c + 1) * P],
+                        rhs=kv_sb[:, b, h * DH : (h + 1) * DH],
+                        start=True,
+                        stop=True,
+                    )
+
+        def divide(s, c, g):
+            b = s // (PAIRS_PER_BLOCK * BLOCKS_PER_SEQ)
+            ctx_sb[s, c, g] = work.tile([P, HALF, ROWS // HALF], BF16, name="ctx_sb", tag="ctx_sb%d" % g)
+            dst = ctx_sb[s, c, g][:].rearrange("p u (h c) -> p h u c", h=HEADS)
+            src = ctx_ps[s, c, g][:].rearrange("p h (u c) -> p h u c", u=HALF)
             head = b * H + g * HEADS
-            if g == 0 and i % VECTOR_TAKES != 0:
+            if g == 0:
                 for hh in range(HEADS):
                     nc.scalar.activation(
                         out=dst[:, hh],
@@ -155,94 +175,106 @@ def tile_linearattention_pb_t_kernel(tc, q_feat, kv, denom, Wo, bo, out):
                     out=dst,
                     in0=src,
                     in1=rden_full[:, head * DH : (head + HEADS) * DH].rearrange(
-                        "p (h u c) -> p h u c", h=HEADS, u=PAIRS
+                        "p (h u c) -> p h u c", h=HEADS, u=HALF
                     ),
                     op=mybir.AluOpType.mult,
                 )
 
-        rden_full = const.tile([P, B * H * DH], F32)
-
-        def transpose_ctx(i):
-            ctxT_ps[i] = ctxT_banks.tile([P, PASSES, PAIRS, P], F32, name="ctxT_ps", tag="ctxT_ps")
+        def transpose_ctx(s, c):
+            ctxT_ps[s, c] = ctxT_banks.tile([P, PASSES, HALF, P], F32, name="ctxT_ps", tag="ctxT_ps")
             for g in range(PASSES):
-                for u in range(PAIRS):
+                for u in range(HALF):
                     nc.tensor.transpose(
-                        ctxT_ps[i][:, g, u, :], ctx_sb[i, g][:, u, :].bitcast(F32), identity_f32[:]
+                        ctxT_ps[s, c][:, g, u, :], ctx_sb[s, c, g][:, u, :].bitcast(F32), identity[:]
                     )
 
-        def regroup(i):
-            grouped[i] = work.tile([P, PASSES, P, PACK], BF16, name="grouped", tag="grouped", align_bytes=64)
+        def regroup(s, c):
+            grouped[s, c] = work.tile([P, PASSES, P, PACK], BF16, name="grouped", tag="grouped", align_bytes=64)
             nc.scalar.copy(
-                out=grouped[i][:].rearrange("p g s t -> p (g s t)").bitcast(F32).rearrange(
-                    "p (g s u) -> p g s u", g=PASSES, u=PAIRS
+                out=grouped[s, c][:].rearrange("p g m t -> p (g m t)").bitcast(F32).rearrange(
+                    "p (g m u) -> p g m u", g=PASSES, u=HALF
                 ),
-                in_=ctxT_ps[i][:].rearrange("p g u s -> p g s u"),
+                in_=ctxT_ps[s, c][:].rearrange("p g u m -> p g m u"),
             )
 
-        def quantise(i):
-            codes[i] = mx_pool.tile([P, PASSES, P], U32, name="codes", tag="codes", align_bytes=64)
-            scales[i] = mx_pool.tile([P, PASSES, P], U8, name="scales", tag="scales", align_bytes=64)
+        def quantise(s, c):
+            codes[s, c] = mx_pool.tile([P, PASSES, P], U32, name="codes", tag="codes", align_bytes=64)
+            scales[s, c] = mx_pool.tile([P, PASSES, P], U8, name="scales", tag="scales", align_bytes=64)
             nc.vector.quantize_mx(
-                out=codes[i][:].rearrange("p g s -> p (g s)").bitcast(FP8X4),
-                scales=scales[i][:].rearrange("p g s -> p (g s)"),
-                in_=grouped[i][:].rearrange("p g s t -> p (g s t)"),
+                out=codes[s, c][:].rearrange("p g m -> p (g m)").bitcast(FP8X4),
+                scales=scales[s, c][:].rearrange("p g m -> p (g m)"),
+                in_=grouped[s, c][:].rearrange("p g m t -> p (g m t)"),
             )
 
-        def project(i):
-            out_ps[i] = out_banks.tile([P, E], F32, name="out_ps", tag="out_ps")
+        def project(s, c):
+            out_ps[s, c] = out_banks.tile([P, E], F32, name="out_ps", tag="out_ps")
             for g in range(PASSES):
                 nc.tensor.matmul_mx(
-                    out=out_ps[i][:],
-                    lhsT=codes[i][:, g, :].bitcast(FP8X4),
-                    lhsT_scale=scales[i][:, g, :],
+                    out=out_ps[s, c][:],
+                    lhsT=codes[s, c][:, g, :].bitcast(FP8X4),
+                    lhsT_scale=scales[s, c][:, g, :],
                     rhs=wo_codes[:, g, :].bitcast(FP8X4),
                     rhs_scale=wo_scales[:, g, :],
                     start=(g == 0),
                     stop=(g == PASSES - 1),
                 )
 
-        def add_bias_and_store(i):
-            out_sb[i] = out_pool.tile([P, E], F32, name="out_sb", tag="out_sb")
-            nc.vector.tensor_tensor(out=out_sb[i][:], in0=out_ps[i][:], in1=bias_sb[:], op=mybir.AluOpType.add)
-            blk, j = divmod(i, J)
+        def add_bias_and_store(s, c):
+            out_sb[s, c] = out_pool.tile([P, E], F32, name="out_sb", tag="out_sb")
+            nc.vector.tensor_tensor(
+                out=out_sb[s, c][:], in0=out_ps[s, c][:], in1=bias_sb[:], op=mybir.AluOpType.add
+            )
+            blk, l = divmod(s, PAIRS_PER_BLOCK)
             b, part = divmod(blk, BLOCKS_PER_SEQ)
-            rows = out[b, part * BLOCK : (part + 1) * BLOCK, :].rearrange("(p j) n -> p j n", j=J)
-            nc.sync.dma_start(out=rows[:, j, :], in_=out_sb[i][:])
+            first = part * BLOCK + c * HALF * P
+            rows = out[b, first : first + HALF * P, :].rearrange("(m l) n -> l m n", l=PAIRS_PER_BLOCK)
+            nc.sync.dma_start(out=rows[l], in_=out_sb[s, c][:])
 
-        for step in range(N_TILES + 6):
+        def is_pair(s):
+            return 0 <= s < N_PAIRS
+
+        for step in range(N_PAIRS + 6):
+            if is_pair(step - 3):
+                divide(step - 3, 1, 0)
+                divide(step - 3, 1, 1)
+            if is_pair(step - 1):
+                transpose_q(step - 1, 0)
+                transpose_q(step - 1, 1)
+            if is_pair(step - 3):
+                transpose_ctx(step - 3, 0)
+                transpose_ctx(step - 3, 1)
+            if is_pair(step - 1):
+                copy_qT(step - 1, 0)
+                copy_qT(step - 1, 1)
+            if is_pair(step - 6):
+                add_bias_and_store(step - 6, 0)
+                add_bias_and_store(step - 6, 1)
+            blk, l = divmod(step - 6, PAIRS_PER_BLOCK)
+            if 0 <= blk and blk + LOADS_AHEAD < N_BLOCKS:
+                load_unit(blk + LOADS_AHEAD, l)
+            if is_pair(step - 4):
+                quantise(step - 4, 0)
+            if is_pair(step - 2):
+                plain_matmuls(step - 2, 0)
+            if is_pair(step - 5):
+                project(step - 5, 0)
+                project(step - 5, 1)
+            if is_pair(step - 2):
+                divide(step - 2, 0, 0)
+                divide(step - 2, 0, 1)
+                plain_matmuls(step - 2, 1)
+            if is_pair(step - 3):
+                regroup(step - 3, 0)
+                regroup(step - 3, 1)
+            if is_pair(step - 4):
+                quantise(step - 4, 1)
+            if is_pair(step):
+                pair_queries(step, 0)
+                pair_queries(step, 1)
             if step == 0:
                 order_kv(0)
-                nc.vector.reciprocal(out=rden[:], in_=denom_bc[:])
-                nc.vector.tensor_copy(
-                    out=rden_full[:].rearrange("p (h e) -> p h e", e=DH),
-                    in_=rden[:].unsqueeze(2).to_broadcast([P, B * H, DH]),
-                )
-            if is_tile(step):
-                transpose_q(step)
-            if is_tile(step - 2):
-                divide(step - 2, 0)
-            if step == 4:
+                prepare_division()
+            if step == 3:
                 prepare_projection()
-            if is_tile(step - 5):
-                quantise(step - 5)
-            if is_tile(step - 4):
-                regroup(step - 4)
-            if is_tile(step - 3):
-                transpose_ctx(step - 3)
-            if is_tile(step - 2):
-                divide(step - 2, 1)
-            if is_tile(step - 6):
-                add_bias_and_store(step - 6)
-            blk, j = divmod(step - 6, J)
-            if j in (0, 2) and 0 <= blk and blk + LOADS_AHEAD < N_BLOCKS:
-                load_unit(blk + LOADS_AHEAD, j // 2)
-            if is_tile(step - 1):
-                plain_matmuls(step - 1, 0)
-            if is_tile(step - 5):
-                project(step - 5)
-            if is_tile(step - 1):
-                plain_matmuls(step - 1, 1)
-            if is_tile(step):
-                copy_qT(step)
             if step == 8:
                 order_kv(1)

@@ -32,8 +32,8 @@ def tile_linearattention_pb_t_kernel(tc, q_feat, kv, denom, Wo, bo, out):
     with ExitStack() as stack:
         const = stack.enter_context(tc.tile_pool(name="const", bufs=1))
         q_pool = stack.enter_context(tc.tile_pool(name="q", bufs=(LOADS_AHEAD + 2) * PASSES))
-        work = stack.enter_context(tc.tile_pool(name="work", bufs=4))
-        mx_pool = stack.enter_context(tc.tile_pool(name="mx", bufs=4))
+        work = stack.enter_context(tc.tile_pool(name="work", bufs=6))
+        mx_pool = stack.enter_context(tc.tile_pool(name="mx", bufs=6))
         out_pool = stack.enter_context(tc.tile_pool(name="outs", bufs=6))
         qT_banks = stack.enter_context(tc.psum_pool(name="qT_banks", bufs=2))
         ctx_banks = stack.enter_context(tc.psum_pool(name="ctx_banks", bufs=2))
@@ -57,11 +57,11 @@ def tile_linearattention_pb_t_kernel(tc, q_feat, kv, denom, Wo, bo, out):
         masks.make_identity(nc, identity[:])
 
         load_unit(0, 0)
+        load_unit(0, 1)
         kv_raw = const.tile([P, B, H * DH], BF16, align_bytes=64)
         nc.sync.dma_start(
             out=kv_raw[:, 0, :].rearrange("d (h e) -> d h e", h=H), in_=kv[0].rearrange("h d e -> d h e")
         )
-        load_unit(0, 1)
         denom_bc = const.tile([P, B * H], BF16)
         nc.sync.dma_start(out=denom_bc[:], in_=denom.rearrange("b h x y -> (b h x y)").partition_broadcast(P))
         nc.sync.dma_start(out=bias_row[0:1, :], in_=bo.rearrange("(o n) -> o n", o=1))
@@ -95,19 +95,22 @@ def tile_linearattention_pb_t_kernel(tc, q_feat, kv, denom, Wo, bo, out):
                 in_=rden[:].unsqueeze(2).to_broadcast([P, B * H, DH]),
             )
 
-        def prepare_projection():
+        def spread_bias():
             bias_ps = out_banks.tile([P, E], F32, name="bias_ps", tag="out_ps")
             nc.tensor.matmul(out=bias_ps[:], lhsT=ones[:], rhs=bias_row[:], start=True, stop=True)
-            nc.vector.tensor_copy(out=bias_sb[:], in_=bias_ps[:])
-            for g in range(PASSES):
-                nc.vector.tensor_copy(
-                    out=wo_grouped[:, g].rearrange("p (c i) t -> p c t i", i=4),
-                    in_=wo_raw[:, g].rearrange("p t (c i) -> p c t i", i=4),
-                )
+            nc.scalar.copy(out=bias_sb[:], in_=bias_ps[:])
+
+        def regroup_wo(g):
+            nc.vector.tensor_copy(
+                out=wo_grouped[:, g].rearrange("p (c i) t -> p c t i", i=4),
+                in_=wo_raw[:, g].rearrange("p t (c i) -> p c t i", i=4),
+            )
+
+        def quantise_wo(g):
             nc.vector.quantize_mx(
-                out=wo_codes[:].rearrange("p g n -> p (g n)").bitcast(FP8X4),
-                scales=wo_scales[:].rearrange("p g n -> p (g n)"),
-                in_=wo_grouped[:].rearrange("p g n t -> p (g n t)"),
+                out=wo_codes[:, g, :].bitcast(FP8X4),
+                scales=wo_scales[:, g, :],
+                in_=wo_grouped[:, g].rearrange("p n t -> p (n t)"),
             )
 
         q_pairs, qT_ps, qT_sb, ctx_ps, ctx_sb, ctxT_ps, grouped = {}, {}, {}, {}, {}, {}, {}
@@ -117,17 +120,18 @@ def tile_linearattention_pb_t_kernel(tc, q_feat, kv, denom, Wo, bo, out):
             blk, l = divmod(s, PAIRS_PER_BLOCK)
             q_pairs[s, g] = work.tile([P, HEADS, DH, HALF], BF16, name="q_pairs", tag="q_pairs", align_bytes=64)
             src = q_tiles[blk, g][:].rearrange("p h (r l d) -> p l h d r", r=HALF, l=PAIRS_PER_BLOCK)[:, l]
-            if g == 0:
-                nc.gpsimd.tensor_scalar(
-                    out=q_pairs[s, g][:],
-                    in0=src,
-                    scalar1=1.0,
-                    scalar2=0.0,
-                    op0=mybir.AluOpType.mult,
-                    op1=mybir.AluOpType.add,
-                )
-            else:
+            if (s, g) == (0, 1):
                 nc.vector.tensor_copy(out=q_pairs[s, g][:], in_=src)
+            else:
+                for h in range(0, HEADS, 2):
+                    nc.gpsimd.tensor_scalar(
+                        out=q_pairs[s, g][:, h : h + 2],
+                        in0=src[:, h : h + 2],
+                        scalar1=1.0,
+                        scalar2=0.0,
+                        op0=mybir.AluOpType.mult,
+                        op1=mybir.AluOpType.add,
+                    )
 
         def transpose_q(s, g):
             qT_ps[s, g] = qT_banks.tile([P, HEADS, P], F32, name="qT_ps", tag="qT_ps")
@@ -142,19 +146,18 @@ def tile_linearattention_pb_t_kernel(tc, q_feat, kv, denom, Wo, bo, out):
                 in_=qT_ps[s, g][:].rearrange("d h p -> d (h p)"),
             )
 
-        def plain_matmuls(s, c):
+        def plain_matmuls(s, c, g):
             b = s // (PAIRS_PER_BLOCK * BLOCKS_PER_SEQ)
-            for g in range(PASSES):
-                ctx_ps[s, c, g] = ctx_banks.tile([P, HEADS, DH], F32, name="ctx_ps", tag="ctx_ps")
-                for hh in range(HEADS):
-                    h = g * HEADS + hh
-                    nc.tensor.matmul(
-                        out=ctx_ps[s, c, g][:, hh, :],
-                        lhsT=qT_sb[s, g][:, hh, c * P : (c + 1) * P],
-                        rhs=kv_sb[:, b, h * DH : (h + 1) * DH],
-                        start=True,
-                        stop=True,
-                    )
+            ctx_ps[s, c, g] = ctx_banks.tile([P, HEADS, DH], F32, name="ctx_ps", tag="ctx_ps")
+            for hh in range(HEADS):
+                h = g * HEADS + hh
+                nc.tensor.matmul(
+                    out=ctx_ps[s, c, g][:, hh, :],
+                    lhsT=qT_sb[s, g][:, hh, c * P : (c + 1) * P],
+                    rhs=kv_sb[:, b, h * DH : (h + 1) * DH],
+                    start=True,
+                    stop=True,
+                )
 
         def divide(s, c, g):
             b = s // (PAIRS_PER_BLOCK * BLOCKS_PER_SEQ)
@@ -230,51 +233,45 @@ def tile_linearattention_pb_t_kernel(tc, q_feat, kv, denom, Wo, bo, out):
             rows = out[b, first : first + HALF * P, :].rearrange("(m l) n -> l m n", l=PAIRS_PER_BLOCK)
             nc.sync.dma_start(out=rows[l], in_=out_sb[s, c][:])
 
-        def is_pair(s):
-            return 0 <= s < N_PAIRS
+        N_TILES = N_PAIRS * HALF
 
-        for step in range(N_PAIRS + 6):
-            if is_pair(step - 3):
-                divide(step - 3, 1, 0)
-                divide(step - 3, 1, 1)
-            if is_pair(step - 1):
-                transpose_q(step - 1, 0)
-                transpose_q(step - 1, 1)
-            if is_pair(step - 3):
-                transpose_ctx(step - 3, 0)
-                transpose_ctx(step - 3, 1)
-            if is_pair(step - 1):
-                copy_qT(step - 1, 0)
-                copy_qT(step - 1, 1)
-            if is_pair(step - 6):
-                add_bias_and_store(step - 6, 0)
-                add_bias_and_store(step - 6, 1)
-            blk, l = divmod(step - 6, PAIRS_PER_BLOCK)
-            if 0 <= blk and blk + LOADS_AHEAD < N_BLOCKS:
-                load_unit(blk + LOADS_AHEAD, l)
-            if is_pair(step - 4):
-                quantise(step - 4, 0)
-            if is_pair(step - 2):
-                plain_matmuls(step - 2, 0)
-            if is_pair(step - 5):
-                project(step - 5, 0)
-                project(step - 5, 1)
-            if is_pair(step - 2):
-                divide(step - 2, 0, 0)
-                divide(step - 2, 0, 1)
-                plain_matmuls(step - 2, 1)
-            if is_pair(step - 3):
-                regroup(step - 3, 0)
-                regroup(step - 3, 1)
-            if is_pair(step - 4):
-                quantise(step - 4, 1)
-            if is_pair(step):
-                pair_queries(step, 0)
-                pair_queries(step, 1)
-            if step == 0:
+        def is_tile(i):
+            return 0 <= i < N_TILES
+
+        for step in range(N_TILES + 7):
+            if is_tile(step - 1):
+                transpose_q(*divmod(step - 1, HALF))
+            if is_tile(step - 5):
+                transpose_ctx(*divmod(step - 5, HALF))
+            if is_tile(step - 1):
+                copy_qT(*divmod(step - 1, HALF))
+            if is_tile(step - 3):
+                plain_matmuls(*divmod(step - 3, HALF), 0)
+                divide(*divmod(step - 3, HALF), 0)
+            if is_tile(step - 7):
+                project(*divmod(step - 7, HALF))
+            if is_tile(step - 3):
+                plain_matmuls(*divmod(step - 3, HALF), 1)
+                divide(*divmod(step - 3, HALF), 1)
+            if is_tile(step - 5):
+                regroup(*divmod(step - 5, HALF))
+            if is_tile(step - 7):
+                add_bias_and_store(*divmod(step - 7, HALF))
+                blk, part_of_block = divmod(step - 7, 2 * HALF)
+                if part_of_block % HALF == 0 and blk + LOADS_AHEAD < N_BLOCKS:
+                    load_unit(blk + LOADS_AHEAD, part_of_block // HALF)
+            if is_tile(step - 5):
+                quantise(*divmod(step - 5, HALF))
+            if is_tile(step):
+                pair_queries(*divmod(step, HALF))
+            if step == 1:
                 order_kv(0)
                 prepare_division()
-            if step == 3:
-                prepare_projection()
-            if step == 8:
+            if step in (3, 4):
+                regroup_wo(step - 3)
+            if step in (5, 6):
+                quantise_wo(step - 5)
+            if step == 5:
+                spread_bias()
+            if step == 12:
                 order_kv(1)

@@ -43,11 +43,14 @@ def tile_linearattention_pb_t_kernel(tc, q_feat, kv, denom, Wo, bo, out):
 
         q_tiles = {}
 
-        def load_unit(blk, g):
+        def load_unit(blk, g, pieces=1):
             b, part = divmod(blk, BLOCKS_PER_SEQ)
             q_tiles[blk, g] = q_pool.tile([P, HEADS, J * DH], BF16, name="q_sb", tag="q_sb")
             rows = q_feat[b, g * HEADS : (g + 1) * HEADS, part * BLOCK : (part + 1) * BLOCK, :]
-            nc.sync.dma_start(out=q_tiles[blk, g][:], in_=rows.rearrange("h (p j) d -> p h (j d)", j=J))
+            rows = rows.rearrange("h (p j) d -> p h (j d)", j=J)
+            n = HEADS // pieces
+            for h in range(0, HEADS, n):
+                nc.sync.dma_start(out=q_tiles[blk, g][:, h : h + n], in_=rows[:, h : h + n])
 
         bias_row = const.tile([P, E], BF16)
         nc.vector.memset(bias_row[:], 0.0)
@@ -56,7 +59,7 @@ def tile_linearattention_pb_t_kernel(tc, q_feat, kv, denom, Wo, bo, out):
         identity = const.tile([P, P], F32)
         masks.make_identity(nc, identity[:])
 
-        load_unit(0, 0)
+        load_unit(0, 0, pieces=2)
         load_unit(0, 1)
         kv_raw = const.tile([P, B, H * DH], BF16, align_bytes=64)
         nc.sync.dma_start(
@@ -64,10 +67,14 @@ def tile_linearattention_pb_t_kernel(tc, q_feat, kv, denom, Wo, bo, out):
         )
         denom_bc = const.tile([P, B * H], BF16)
         nc.sync.dma_start(out=denom_bc[:], in_=denom.rearrange("b h x y -> (b h x y)").partition_broadcast(P))
+        wo_raw = [const.tile([P, PACK, E], BF16, name="wo_raw", tag="wo_raw%d" % g) for g in range(PASSES)]
+        for g in range(PASSES):
+            load_unit(1, g)
+            nc.sync.dma_start(
+                out=wo_raw[g][:], in_=Wo[g * ROWS : (g + 1) * ROWS, :].rearrange("(p t) n -> p t n", t=PACK)
+            )
         nc.sync.dma_start(out=bias_row[0:1, :], in_=bo.rearrange("(o n) -> o n", o=1))
-        wo_raw = const.tile([P, PASSES, PACK, E], BF16)
-        nc.sync.dma_start(out=wo_raw[:], in_=Wo.rearrange("(g p t) n -> p g t n", p=P, t=PACK))
-        for blk in range(1, LOADS_AHEAD):
+        for blk in range(2, LOADS_AHEAD):
             load_unit(blk, 0)
             load_unit(blk, 1)
         nc.sync.dma_start(
@@ -103,7 +110,7 @@ def tile_linearattention_pb_t_kernel(tc, q_feat, kv, denom, Wo, bo, out):
         def regroup_wo(g):
             nc.vector.tensor_copy(
                 out=wo_grouped[:, g].rearrange("p (c i) t -> p c t i", i=4),
-                in_=wo_raw[:, g].rearrange("p t (c i) -> p c t i", i=4),
+                in_=wo_raw[g][:].rearrange("p t (c i) -> p c t i", i=4),
             )
 
         def quantise_wo(g):
@@ -120,8 +127,9 @@ def tile_linearattention_pb_t_kernel(tc, q_feat, kv, denom, Wo, bo, out):
             blk, l = divmod(s, PAIRS_PER_BLOCK)
             q_pairs[s, g] = work.tile([P, HEADS, DH, HALF], BF16, name="q_pairs", tag="q_pairs", align_bytes=64)
             src = q_tiles[blk, g][:].rearrange("p h (r l d) -> p l h d r", r=HALF, l=PAIRS_PER_BLOCK)[:, l]
-            if (s, g) == (0, 1):
-                nc.vector.tensor_copy(out=q_pairs[s, g][:], in_=src)
+            if s == 0 or (s % 2 == 1 and g == 1):
+                for h in range(0, HEADS, 2):
+                    nc.vector.tensor_copy(out=q_pairs[s, g][:, h : h + 2], in_=src[:, h : h + 2])
             else:
                 for h in range(0, HEADS, 2):
                     nc.gpsimd.tensor_scalar(

@@ -22,6 +22,7 @@ BLOCKS_PER_SEQ = S // BLOCK
 N_BLOCKS = B * BLOCKS_PER_SEQ
 PAIRS_PER_BLOCK = 2
 N_PAIRS = N_BLOCKS * PAIRS_PER_BLOCK
+FIRST_TILES = 3
 LOADS_AHEAD = 4
 
 FLOPS = 2 * B * H * S * DH * DH + 2 * B * S * H * DH * E
@@ -54,19 +55,20 @@ def tile_linearattention_pb_t_kernel(tc, q_feat, kv, denom, Wo, bo, out):
 
         bias_row = const.tile([P, E], BF16)
         nc.vector.memset(bias_row[:], 0.0)
+        denom_row = const.tile([P, B * H], BF16)
+        nc.vector.memset(denom_row[:], 0.0)
         ones = const.tile([P, P], BF16)
         nc.vector.memset(ones[:], 1.0)
         identity = const.tile([P, P], F32)
         masks.make_identity(nc, identity[:])
 
         load_unit(0, 0, pieces=2)
+        nc.sync.dma_start(out=denom_row[0:1, :], in_=denom.rearrange("b h x y -> (x y) (b h)"))
         load_unit(0, 1)
         kv_raw = const.tile([P, B, H * DH], BF16, align_bytes=64)
         nc.sync.dma_start(
             out=kv_raw[:, 0, :].rearrange("d (h e) -> d h e", h=H), in_=kv[0].rearrange("h d e -> d h e")
         )
-        denom_bc = const.tile([P, B * H], BF16)
-        nc.sync.dma_start(out=denom_bc[:], in_=denom.rearrange("b h x y -> (b h x y)").partition_broadcast(P))
         wo_raw = [const.tile([P, PACK, E], BF16, name="wo_raw", tag="wo_raw%d" % g) for g in range(PASSES)]
         for g in range(PASSES):
             load_unit(1, g)
@@ -83,11 +85,10 @@ def tile_linearattention_pb_t_kernel(tc, q_feat, kv, denom, Wo, bo, out):
 
         kv_sb = const.tile([P, B, H * DH], BF16, align_bytes=64)
         rden = const.tile([P, B * H], F32)
-        rden_full = const.tile([P, B * H * DH], F32)
         bias_sb = const.tile([P, E], F32)
         wo_grouped = const.tile([P, PASSES, E, PACK], BF16, align_bytes=64)
-        wo_codes = const.tile([P, PASSES, E], U32, align_bytes=64)
-        wo_scales = const.tile([P, PASSES, E], U8, align_bytes=64)
+        wo_codes = const.tile([P, PASSES, E], U32, align_bytes=256)
+        wo_scales = const.tile([P, PASSES, E], U8, align_bytes=256)
 
         def order_kv(b):
             nc.vector.tensor_copy(
@@ -95,17 +96,10 @@ def tile_linearattention_pb_t_kernel(tc, q_feat, kv, denom, Wo, bo, out):
                 in_=kv_raw[:, b, :].bitcast(F32).rearrange("d (h c u) -> d h u c", h=H, u=HALF),
             )
 
-        def prepare_division():
-            nc.vector.reciprocal(out=rden[:], in_=denom_bc[:])
-            nc.vector.tensor_copy(
-                out=rden_full[:].rearrange("p (h e) -> p h e", e=DH),
-                in_=rden[:].unsqueeze(2).to_broadcast([P, B * H, DH]),
-            )
-
-        def spread_bias():
-            bias_ps = out_banks.tile([P, E], F32, name="bias_ps", tag="out_ps")
-            nc.tensor.matmul(out=bias_ps[:], lhsT=ones[:], rhs=bias_row[:], start=True, stop=True)
-            nc.scalar.copy(out=bias_sb[:], in_=bias_ps[:])
+        def spread_row(row):
+            spread_ps = out_banks.tile([P, row.shape[1]], F32, name="spread_ps", tag="out_ps")
+            nc.tensor.matmul(out=spread_ps[:], lhsT=ones[:], rhs=row[:], start=True, stop=True)
+            return spread_ps
 
         def regroup_wo(g):
             nc.vector.tensor_copy(
@@ -127,7 +121,7 @@ def tile_linearattention_pb_t_kernel(tc, q_feat, kv, denom, Wo, bo, out):
             blk, l = divmod(s, PAIRS_PER_BLOCK)
             q_pairs[s, g] = work.tile([P, HEADS, DH, HALF], BF16, name="q_pairs", tag="q_pairs", align_bytes=64)
             src = q_tiles[blk, g][:].rearrange("p h (r l d) -> p l h d r", r=HALF, l=PAIRS_PER_BLOCK)[:, l]
-            if s == 0 or (s % 2 == 1 and g == 1):
+            if s == 0 or (s, g) == (1, 1):
                 for h in range(0, HEADS, 2):
                     nc.vector.tensor_copy(out=q_pairs[s, g][:, h : h + 2], in_=src[:, h : h + 2])
             else:
@@ -173,7 +167,7 @@ def tile_linearattention_pb_t_kernel(tc, q_feat, kv, denom, Wo, bo, out):
             dst = ctx_sb[s, c, g][:].rearrange("p u (h c) -> p h u c", h=HEADS)
             src = ctx_ps[s, c, g][:].rearrange("p h (u c) -> p h u c", u=HALF)
             head = b * H + g * HEADS
-            if g == 0:
+            if g == 0 and 2 * s + c >= FIRST_TILES:
                 for hh in range(HEADS):
                     nc.scalar.activation(
                         out=dst[:, hh],
@@ -185,9 +179,7 @@ def tile_linearattention_pb_t_kernel(tc, q_feat, kv, denom, Wo, bo, out):
                 nc.vector.tensor_tensor(
                     out=dst,
                     in0=src,
-                    in1=rden_full[:, head * DH : (head + HEADS) * DH].rearrange(
-                        "p (h u c) -> p h u c", h=HEADS, u=HALF
-                    ),
+                    in1=rden[:, head : head + HEADS].unsqueeze(2).unsqueeze(3).to_broadcast([P, HEADS, HALF, DH // HALF]),
                     op=mybir.AluOpType.mult,
                 )
 
@@ -209,8 +201,8 @@ def tile_linearattention_pb_t_kernel(tc, q_feat, kv, denom, Wo, bo, out):
             )
 
         def quantise(s, c):
-            codes[s, c] = mx_pool.tile([P, PASSES, P], U32, name="codes", tag="codes", align_bytes=64)
-            scales[s, c] = mx_pool.tile([P, PASSES, P], U8, name="scales", tag="scales", align_bytes=64)
+            codes[s, c] = mx_pool.tile([P, PASSES, P], U32, name="codes", tag="codes", align_bytes=256)
+            scales[s, c] = mx_pool.tile([P, PASSES, P], U8, name="scales", tag="scales", align_bytes=256)
             nc.vector.quantize_mx(
                 out=codes[s, c][:].rearrange("p g m -> p (g m)").bitcast(FP8X4),
                 scales=scales[s, c][:].rearrange("p g m -> p (g m)"),
@@ -270,16 +262,18 @@ def tile_linearattention_pb_t_kernel(tc, q_feat, kv, denom, Wo, bo, out):
                     load_unit(blk + LOADS_AHEAD, part_of_block // HALF)
             if is_tile(step - 5):
                 quantise(*divmod(step - 5, HALF))
-            if is_tile(step):
-                pair_queries(*divmod(step, HALF))
+            for j in (0, 1) if step == 0 else (step + 1,):
+                if is_tile(j):
+                    pair_queries(*divmod(j, HALF))
             if step == 1:
                 order_kv(0)
-                prepare_division()
+            if step == 2:
+                nc.vector.reciprocal(out=rden[:], in_=spread_row(denom_row)[:])
             if step in (3, 4):
                 regroup_wo(step - 3)
             if step in (5, 6):
                 quantise_wo(step - 5)
             if step == 5:
-                spread_bias()
+                nc.scalar.copy(out=bias_sb[:], in_=spread_row(bias_row)[:])
             if step == 12:
                 order_kv(1)

@@ -22,7 +22,8 @@ BLOCKS_PER_SEQ = S // BLOCK
 N_BLOCKS = B * BLOCKS_PER_SEQ
 PAIRS_PER_BLOCK = 2
 N_PAIRS = N_BLOCKS * PAIRS_PER_BLOCK
-FIRST_TILES = 3
+FIRST_TILES = 2
+DIRECT_PAIRS = 4
 LOADS_AHEAD = 4
 
 FLOPS = 2 * B * H * S * DH * DH + 2 * B * S * H * DH * E
@@ -44,14 +45,14 @@ def tile_linearattention_pb_t_kernel(tc, q_feat, kv, denom, Wo, bo, out):
 
         q_tiles = {}
 
-        def load_unit(blk, g, pieces=1):
+        def load_unit(blk, g, first_j=0, last_j=J):
             b, part = divmod(blk, BLOCKS_PER_SEQ)
-            q_tiles[blk, g] = q_pool.tile([P, HEADS, J * DH], BF16, name="q_sb", tag="q_sb")
+            if first_j == 0:
+                q_tiles[blk, g] = q_pool.tile([P, HEADS, J * DH], BF16, name="q_sb", tag="q_sb")
             rows = q_feat[b, g * HEADS : (g + 1) * HEADS, part * BLOCK : (part + 1) * BLOCK, :]
             rows = rows.rearrange("h (p j) d -> p h (j d)", j=J)
-            n = HEADS // pieces
-            for h in range(0, HEADS, n):
-                nc.sync.dma_start(out=q_tiles[blk, g][:, h : h + n], in_=rows[:, h : h + n])
+            cols = slice(first_j * DH, last_j * DH)
+            nc.sync.dma_start(out=q_tiles[blk, g][:, :, cols], in_=rows[:, :, cols])
 
         bias_row = const.tile([P, E], BF16)
         nc.vector.memset(bias_row[:], 0.0)
@@ -59,22 +60,28 @@ def tile_linearattention_pb_t_kernel(tc, q_feat, kv, denom, Wo, bo, out):
         nc.vector.memset(denom_row[:], 0.0)
         ones = const.tile([P, P], BF16)
         nc.vector.memset(ones[:], 1.0)
+        identity_bf16 = const.tile([P, P], BF16)
+        masks.make_identity(nc, identity_bf16[:])
         identity = const.tile([P, P], F32)
         masks.make_identity(nc, identity[:])
 
-        load_unit(0, 0, pieces=2)
+        load_unit(0, 0, last_j=HALF)
+        load_unit(0, 1, last_j=HALF)
         nc.sync.dma_start(out=denom_row[0:1, :], in_=denom.rearrange("b h x y -> (x y) (b h)"))
-        load_unit(0, 1)
         kv_raw = const.tile([P, B, H * DH], BF16, align_bytes=64)
         nc.sync.dma_start(
             out=kv_raw[:, 0, :].rearrange("d (h e) -> d h e", h=H), in_=kv[0].rearrange("h d e -> d h e")
         )
+        load_unit(0, 0, first_j=HALF)
+        load_unit(0, 1, first_j=HALF)
         wo_raw = [const.tile([P, PACK, E], BF16, name="wo_raw", tag="wo_raw%d" % g) for g in range(PASSES)]
         for g in range(PASSES):
-            load_unit(1, g)
             nc.sync.dma_start(
                 out=wo_raw[g][:], in_=Wo[g * ROWS : (g + 1) * ROWS, :].rearrange("(p t) n -> p t n", t=PACK)
             )
+            if g == 0:
+                load_unit(1, 0)
+                load_unit(1, 1)
         nc.sync.dma_start(out=bias_row[0:1, :], in_=bo.rearrange("(o n) -> o n", o=1))
         for blk in range(2, LOADS_AHEAD):
             load_unit(blk, 0)
@@ -101,11 +108,19 @@ def tile_linearattention_pb_t_kernel(tc, q_feat, kv, denom, Wo, bo, out):
             nc.tensor.matmul(out=spread_ps[:], lhsT=ones[:], rhs=row[:], start=True, stop=True)
             return spread_ps
 
-        def regroup_wo(g):
-            nc.vector.tensor_copy(
-                out=wo_grouped[:, g].rearrange("p (c i) t -> p c t i", i=4),
-                in_=wo_raw[g][:].rearrange("p t (c i) -> p c t i", i=4),
+        def copy_on_gpsimd(dst, src):
+            nc.gpsimd.tensor_scalar(
+                out=dst, in0=src, scalar1=1.0, scalar2=0.0, op0=mybir.AluOpType.mult, op1=mybir.AluOpType.add
             )
+
+        def regroup_wo(g):
+            if g == 0:
+                copy_on_gpsimd(wo_grouped[:, g], wo_raw[g][:].rearrange("p t n -> p n t"))
+            else:
+                nc.vector.tensor_copy(
+                    out=wo_grouped[:, g].rearrange("p (c i) t -> p c t i", i=4),
+                    in_=wo_raw[g][:].rearrange("p t (c i) -> p c t i", i=4),
+                )
 
         def quantise_wo(g):
             nc.vector.quantize_mx(
@@ -118,24 +133,27 @@ def tile_linearattention_pb_t_kernel(tc, q_feat, kv, denom, Wo, bo, out):
         codes, scales, out_ps, out_sb = {}, {}, {}, {}
 
         def pair_queries(s, g):
+            if s < DIRECT_PAIRS:
+                return
             blk, l = divmod(s, PAIRS_PER_BLOCK)
             q_pairs[s, g] = work.tile([P, HEADS, DH, HALF], BF16, name="q_pairs", tag="q_pairs", align_bytes=64)
             src = q_tiles[blk, g][:].rearrange("p h (r l d) -> p l h d r", r=HALF, l=PAIRS_PER_BLOCK)[:, l]
-            if s == 0 or (s, g) == (1, 1):
-                for h in range(0, HEADS, 2):
-                    nc.vector.tensor_copy(out=q_pairs[s, g][:, h : h + 2], in_=src[:, h : h + 2])
-            else:
-                for h in range(0, HEADS, 2):
-                    nc.gpsimd.tensor_scalar(
-                        out=q_pairs[s, g][:, h : h + 2],
-                        in0=src[:, h : h + 2],
-                        scalar1=1.0,
-                        scalar2=0.0,
-                        op0=mybir.AluOpType.mult,
-                        op1=mybir.AluOpType.add,
-                    )
+            for h in range(0, HEADS, 2):
+                copy_on_gpsimd(q_pairs[s, g][:, h : h + 2], src[:, h : h + 2])
 
         def transpose_q(s, g):
+            if s < DIRECT_PAIRS:
+                blk, l = divmod(s, PAIRS_PER_BLOCK)
+                qT_ps[s, g] = qT_banks.tile([P, HEADS, HALF, P], BF16, name="qT_ps", tag="qT_ps")
+                for hh in range(HEADS):
+                    for c in range(HALF):
+                        j = HALF * l + c
+                        nc.tensor.transpose(
+                            qT_ps[s, g][:, hh, c, :],
+                            q_tiles[blk, g][:, hh, j * DH : (j + 1) * DH],
+                            identity_bf16[:],
+                        )
+                return
             qT_ps[s, g] = qT_banks.tile([P, HEADS, P], F32, name="qT_ps", tag="qT_ps")
             words = q_pairs[s, g][:].rearrange("p h d r -> p (h d r)").bitcast(F32)
             for hh in range(HEADS):
@@ -145,7 +163,11 @@ def tile_linearattention_pb_t_kernel(tc, q_feat, kv, denom, Wo, bo, out):
             qT_sb[s, g] = work.tile([P, HEADS, HALF * P], BF16, name="qT_sb", tag="qT_sb", align_bytes=64)
             nc.scalar.copy(
                 out=qT_sb[s, g][:].rearrange("d h m -> d (h m)").bitcast(F32),
-                in_=qT_ps[s, g][:].rearrange("d h p -> d (h p)"),
+                in_=(
+                    qT_ps[s, g][:].rearrange("d h c m -> d (h c m)").bitcast(F32)
+                    if s < DIRECT_PAIRS
+                    else qT_ps[s, g][:].rearrange("d h p -> d (h p)")
+                ),
             )
 
         def plain_matmuls(s, c, g):
@@ -229,9 +251,13 @@ def tile_linearattention_pb_t_kernel(tc, q_feat, kv, denom, Wo, bo, out):
             )
             blk, l = divmod(s, PAIRS_PER_BLOCK)
             b, part = divmod(blk, BLOCKS_PER_SEQ)
-            first = part * BLOCK + c * HALF * P
-            rows = out[b, first : first + HALF * P, :].rearrange("(m l) n -> l m n", l=PAIRS_PER_BLOCK)
-            nc.sync.dma_start(out=rows[l], in_=out_sb[s, c][:])
+            if s < DIRECT_PAIRS:
+                rows = out[b, part * BLOCK : (part + 1) * BLOCK, :].rearrange("(m j) n -> j m n", j=J)
+                nc.sync.dma_start(out=rows[HALF * l + c], in_=out_sb[s, c][:])
+            else:
+                first = part * BLOCK + c * HALF * P
+                rows = out[b, first : first + HALF * P, :].rearrange("(m l) n -> l m n", l=PAIRS_PER_BLOCK)
+                nc.sync.dma_start(out=rows[l], in_=out_sb[s, c][:])
 
         N_TILES = N_PAIRS * HALF
 
@@ -269,8 +295,8 @@ def tile_linearattention_pb_t_kernel(tc, q_feat, kv, denom, Wo, bo, out):
                 order_kv(0)
             if step == 2:
                 nc.vector.reciprocal(out=rden[:], in_=spread_row(denom_row)[:])
-            if step in (3, 4):
-                regroup_wo(step - 3)
+            if step in (3, 5):
+                regroup_wo(step // 4)
             if step in (5, 6):
                 quantise_wo(step - 5)
             if step == 5:

from contextlib import ExitStack

import concourse.masks as masks
import concourse.mybir as mybir

BF16 = mybir.dt.bfloat16
F32 = mybir.dt.float32
U32 = mybir.dt.uint32
U8 = mybir.dt.uint8
FP8X4 = mybir.dt.float8_e4m3fn_x4

P = 128
B, H, S, DH, E = 2, 8, 4096, 128, 512
PACK = 4
HALF = 2
HEADS = 4
PASSES = H // HEADS
ROWS = HEADS * DH
J = 4
BLOCK = P * J
BLOCKS_PER_SEQ = S // BLOCK
N_BLOCKS = B * BLOCKS_PER_SEQ
PAIRS_PER_BLOCK = 2
N_PAIRS = N_BLOCKS * PAIRS_PER_BLOCK
FIRST_TILES = 2
DIRECT_PAIRS = 4
LOADS_AHEAD = 4

FLOPS = 2 * B * H * S * DH * DH + 2 * B * S * H * DH * E


def tile_linearattention_pb_t_kernel(tc, q_feat, kv, denom, Wo, bo, out):
    nc = tc.nc
    with ExitStack() as stack:
        const = stack.enter_context(tc.tile_pool(name="const", bufs=1))
        q_pool = stack.enter_context(tc.tile_pool(name="q", bufs=(LOADS_AHEAD + 2) * PASSES))
        work = stack.enter_context(tc.tile_pool(name="work", bufs=6))
        mx_pool = stack.enter_context(tc.tile_pool(name="mx", bufs=6))
        out_pool = stack.enter_context(tc.tile_pool(name="outs", bufs=6))
        qT_banks = stack.enter_context(tc.psum_pool(name="qT_banks", bufs=2))
        ctx_banks = stack.enter_context(tc.psum_pool(name="ctx_banks", bufs=2))
        ctxT_banks = stack.enter_context(tc.psum_pool(name="ctxT_banks", bufs=2))
        out_banks = stack.enter_context(tc.psum_pool(name="out_banks", bufs=2))
        stack.enter_context(tc.manual_schedule())

        q_tiles = {}

        def load_unit(blk, g, first_j=0, last_j=J):
            b, part = divmod(blk, BLOCKS_PER_SEQ)
            if first_j == 0:
                q_tiles[blk, g] = q_pool.tile([P, HEADS, J * DH], BF16, name="q_sb", tag="q_sb")
            rows = q_feat[b, g * HEADS : (g + 1) * HEADS, part * BLOCK : (part + 1) * BLOCK, :]
            rows = rows.rearrange("h (p j) d -> p h (j d)", j=J)
            cols = slice(first_j * DH, last_j * DH)
            nc.sync.dma_start(out=q_tiles[blk, g][:, :, cols], in_=rows[:, :, cols])

        bias_row = const.tile([P, E], BF16)
        nc.vector.memset(bias_row[:], 0.0)
        denom_row = const.tile([P, B * H], BF16)
        nc.vector.memset(denom_row[:], 0.0)
        ones = const.tile([P, P], BF16)
        nc.vector.memset(ones[:], 1.0)
        identity_bf16 = const.tile([P, P], BF16)
        masks.make_identity(nc, identity_bf16[:])
        identity = const.tile([P, P], F32)
        masks.make_identity(nc, identity[:])

        load_unit(0, 0, last_j=HALF)
        load_unit(0, 1, last_j=HALF)
        nc.sync.dma_start(out=denom_row[0:1, :], in_=denom.rearrange("b h x y -> (x y) (b h)"))
        kv_raw = const.tile([P, B, H * DH], BF16, align_bytes=64)
        nc.sync.dma_start(
            out=kv_raw[:, 0, :].rearrange("d (h e) -> d h e", h=H), in_=kv[0].rearrange("h d e -> d h e")
        )
        load_unit(0, 0, first_j=HALF)
        load_unit(0, 1, first_j=HALF)
        wo_raw = [const.tile([P, PACK, E], BF16, name="wo_raw", tag="wo_raw%d" % g) for g in range(PASSES)]
        for g in range(PASSES):
            nc.sync.dma_start(
                out=wo_raw[g][:], in_=Wo[g * ROWS : (g + 1) * ROWS, :].rearrange("(p t) n -> p t n", t=PACK)
            )
            if g == 0:
                load_unit(1, 0)
                load_unit(1, 1)
        nc.sync.dma_start(out=bias_row[0:1, :], in_=bo.rearrange("(o n) -> o n", o=1))
        for blk in range(2, LOADS_AHEAD):
            load_unit(blk, 0)
            load_unit(blk, 1)
        nc.sync.dma_start(
            out=kv_raw[:, 1, :].rearrange("d (h e) -> d h e", h=H), in_=kv[1].rearrange("h d e -> d h e")
        )

        kv_sb = const.tile([P, B, H * DH], BF16, align_bytes=64)
        rden = const.tile([P, B * H], F32)
        bias_sb = const.tile([P, E], F32)
        wo_grouped = const.tile([P, PASSES, E, PACK], BF16, align_bytes=64)
        wo_codes = const.tile([P, PASSES, E], U32, align_bytes=256)
        wo_scales = const.tile([P, PASSES, E], U8, align_bytes=256)

        def order_kv(b):
            nc.vector.tensor_copy(
                out=kv_sb[:, b, :].bitcast(F32).rearrange("d (h u c) -> d h u c", h=H, u=HALF),
                in_=kv_raw[:, b, :].bitcast(F32).rearrange("d (h c u) -> d h u c", h=H, u=HALF),
            )

        def spread_row(row):
            spread_ps = out_banks.tile([P, row.shape[1]], F32, name="spread_ps", tag="out_ps")
            nc.tensor.matmul(out=spread_ps[:], lhsT=ones[:], rhs=row[:], start=True, stop=True)
            return spread_ps

        def copy_on_gpsimd(dst, src):
            nc.gpsimd.tensor_scalar(
                out=dst, in0=src, scalar1=1.0, scalar2=0.0, op0=mybir.AluOpType.mult, op1=mybir.AluOpType.add
            )

        def regroup_wo(g):
            if g == 0:
                copy_on_gpsimd(wo_grouped[:, g], wo_raw[g][:].rearrange("p t n -> p n t"))
            else:
                nc.vector.tensor_copy(
                    out=wo_grouped[:, g].rearrange("p (c i) t -> p c t i", i=4),
                    in_=wo_raw[g][:].rearrange("p t (c i) -> p c t i", i=4),
                )

        def quantise_wo(g):
            nc.vector.quantize_mx(
                out=wo_codes[:, g, :].bitcast(FP8X4),
                scales=wo_scales[:, g, :],
                in_=wo_grouped[:, g].rearrange("p n t -> p (n t)"),
            )

        q_pairs, qT_ps, qT_sb, ctx_ps, ctx_sb, ctxT_ps, grouped = {}, {}, {}, {}, {}, {}, {}
        codes, scales, out_ps, out_sb = {}, {}, {}, {}

        def pair_queries(s, g):
            if s < DIRECT_PAIRS:
                return
            blk, l = divmod(s, PAIRS_PER_BLOCK)
            q_pairs[s, g] = work.tile([P, HEADS, DH, HALF], BF16, name="q_pairs", tag="q_pairs", align_bytes=64)
            src = q_tiles[blk, g][:].rearrange("p h (r l d) -> p l h d r", r=HALF, l=PAIRS_PER_BLOCK)[:, l]
            for h in range(0, HEADS, 2):
                copy_on_gpsimd(q_pairs[s, g][:, h : h + 2], src[:, h : h + 2])

        def transpose_q(s, g):
            if s < DIRECT_PAIRS:
                blk, l = divmod(s, PAIRS_PER_BLOCK)
                qT_ps[s, g] = qT_banks.tile([P, HEADS, HALF, P], BF16, name="qT_ps", tag="qT_ps")
                for hh in range(HEADS):
                    for c in range(HALF):
                        j = HALF * l + c
                        nc.tensor.transpose(
                            qT_ps[s, g][:, hh, c, :],
                            q_tiles[blk, g][:, hh, j * DH : (j + 1) * DH],
                            identity_bf16[:],
                        )
                return
            qT_ps[s, g] = qT_banks.tile([P, HEADS, P], F32, name="qT_ps", tag="qT_ps")
            words = q_pairs[s, g][:].rearrange("p h d r -> p (h d r)").bitcast(F32)
            for hh in range(HEADS):
                nc.tensor.transpose(qT_ps[s, g][:, hh, :], words[:, hh * P : (hh + 1) * P], identity[:])

        def copy_qT(s, g):
            qT_sb[s, g] = work.tile([P, HEADS, HALF * P], BF16, name="qT_sb", tag="qT_sb", align_bytes=64)
            nc.scalar.copy(
                out=qT_sb[s, g][:].rearrange("d h m -> d (h m)").bitcast(F32),
                in_=(
                    qT_ps[s, g][:].rearrange("d h c m -> d (h c m)").bitcast(F32)
                    if s < DIRECT_PAIRS
                    else qT_ps[s, g][:].rearrange("d h p -> d (h p)")
                ),
            )

        def plain_matmuls(s, c, g):
            b = s // (PAIRS_PER_BLOCK * BLOCKS_PER_SEQ)
            ctx_ps[s, c, g] = ctx_banks.tile([P, HEADS, DH], F32, name="ctx_ps", tag="ctx_ps")
            for hh in range(HEADS):
                h = g * HEADS + hh
                nc.tensor.matmul(
                    out=ctx_ps[s, c, g][:, hh, :],
                    lhsT=qT_sb[s, g][:, hh, c * P : (c + 1) * P],
                    rhs=kv_sb[:, b, h * DH : (h + 1) * DH],
                    start=True,
                    stop=True,
                )

        def divide(s, c, g):
            b = s // (PAIRS_PER_BLOCK * BLOCKS_PER_SEQ)
            ctx_sb[s, c, g] = work.tile([P, HALF, ROWS // HALF], BF16, name="ctx_sb", tag="ctx_sb%d" % g)
            dst = ctx_sb[s, c, g][:].rearrange("p u (h c) -> p h u c", h=HEADS)
            src = ctx_ps[s, c, g][:].rearrange("p h (u c) -> p h u c", u=HALF)
            head = b * H + g * HEADS
            if g == 0 and 2 * s + c >= FIRST_TILES:
                for hh in range(HEADS):
                    nc.scalar.activation(
                        out=dst[:, hh],
                        in_=src[:, hh],
                        func=mybir.ActivationFunctionType.Copy,
                        scale=rden[:, head + hh : head + hh + 1],
                    )
            else:
                nc.vector.tensor_tensor(
                    out=dst,
                    in0=src,
                    in1=rden[:, head : head + HEADS].unsqueeze(2).unsqueeze(3).to_broadcast([P, HEADS, HALF, DH // HALF]),
                    op=mybir.AluOpType.mult,
                )

        def transpose_ctx(s, c):
            ctxT_ps[s, c] = ctxT_banks.tile([P, PASSES, HALF, P], F32, name="ctxT_ps", tag="ctxT_ps")
            for g in range(PASSES):
                for u in range(HALF):
                    nc.tensor.transpose(
                        ctxT_ps[s, c][:, g, u, :], ctx_sb[s, c, g][:, u, :].bitcast(F32), identity[:]
                    )

        def regroup(s, c):
            grouped[s, c] = work.tile([P, PASSES, P, PACK], BF16, name="grouped", tag="grouped", align_bytes=64)
            nc.scalar.copy(
                out=grouped[s, c][:].rearrange("p g m t -> p (g m t)").bitcast(F32).rearrange(
                    "p (g m u) -> p g m u", g=PASSES, u=HALF
                ),
                in_=ctxT_ps[s, c][:].rearrange("p g u m -> p g m u"),
            )

        def quantise(s, c):
            codes[s, c] = mx_pool.tile([P, PASSES, P], U32, name="codes", tag="codes", align_bytes=256)
            scales[s, c] = mx_pool.tile([P, PASSES, P], U8, name="scales", tag="scales", align_bytes=256)
            nc.vector.quantize_mx(
                out=codes[s, c][:].rearrange("p g m -> p (g m)").bitcast(FP8X4),
                scales=scales[s, c][:].rearrange("p g m -> p (g m)"),
                in_=grouped[s, c][:].rearrange("p g m t -> p (g m t)"),
            )

        def project(s, c):
            out_ps[s, c] = out_banks.tile([P, E], F32, name="out_ps", tag="out_ps")
            for g in range(PASSES):
                nc.tensor.matmul_mx(
                    out=out_ps[s, c][:],
                    lhsT=codes[s, c][:, g, :].bitcast(FP8X4),
                    lhsT_scale=scales[s, c][:, g, :],
                    rhs=wo_codes[:, g, :].bitcast(FP8X4),
                    rhs_scale=wo_scales[:, g, :],
                    start=(g == 0),
                    stop=(g == PASSES - 1),
                )

        def add_bias_and_store(s, c):
            out_sb[s, c] = out_pool.tile([P, E], F32, name="out_sb", tag="out_sb")
            nc.vector.tensor_tensor(
                out=out_sb[s, c][:], in0=out_ps[s, c][:], in1=bias_sb[:], op=mybir.AluOpType.add
            )
            blk, l = divmod(s, PAIRS_PER_BLOCK)
            b, part = divmod(blk, BLOCKS_PER_SEQ)
            if s < DIRECT_PAIRS:
                rows = out[b, part * BLOCK : (part + 1) * BLOCK, :].rearrange("(m j) n -> j m n", j=J)
                nc.sync.dma_start(out=rows[HALF * l + c], in_=out_sb[s, c][:])
            else:
                first = part * BLOCK + c * HALF * P
                rows = out[b, first : first + HALF * P, :].rearrange("(m l) n -> l m n", l=PAIRS_PER_BLOCK)
                nc.sync.dma_start(out=rows[l], in_=out_sb[s, c][:])

        N_TILES = N_PAIRS * HALF

        def is_tile(i):
            return 0 <= i < N_TILES

        for step in range(N_TILES + 7):
            if is_tile(step - 1):
                transpose_q(*divmod(step - 1, HALF))
            if is_tile(step - 5):
                transpose_ctx(*divmod(step - 5, HALF))
            if is_tile(step - 1):
                copy_qT(*divmod(step - 1, HALF))
            if is_tile(step - 3):
                plain_matmuls(*divmod(step - 3, HALF), 0)
                divide(*divmod(step - 3, HALF), 0)
            if is_tile(step - 7):
                project(*divmod(step - 7, HALF))
            if is_tile(step - 3):
                plain_matmuls(*divmod(step - 3, HALF), 1)
                divide(*divmod(step - 3, HALF), 1)
            if is_tile(step - 5):
                regroup(*divmod(step - 5, HALF))
            if is_tile(step - 7):
                add_bias_and_store(*divmod(step - 7, HALF))
                blk, part_of_block = divmod(step - 7, 2 * HALF)
                if part_of_block % HALF == 0 and blk + LOADS_AHEAD < N_BLOCKS:
                    load_unit(blk + LOADS_AHEAD, part_of_block // HALF)
            if is_tile(step - 5):
                quantise(*divmod(step - 5, HALF))
            for j in (0, 1) if step == 0 else (step + 1,):
                if is_tile(j):
                    pair_queries(*divmod(j, HALF))
            if step == 1:
                order_kv(0)
            if step == 2:
                nc.vector.reciprocal(out=rden[:], in_=spread_row(denom_row)[:])
            if step in (3, 5):
                regroup_wo(step // 4)
            if step in (5, 6):
                quantise_wo(step - 5)
            if step == 5:
                nc.scalar.copy(out=bias_sb[:], in_=spread_row(bias_row)[:])
            if step == 12:
                order_kv(1)
